import numpy as np
import ml_dtypes


def mxq(x, axis, fmt="e4m3"):
    dtype, down = {"e4m3": (ml_dtypes.float8_e4m3fn, 7), "e5m2": (ml_dtypes.float8_e5m2, 14)}[fmt]
    v = np.moveaxis(np.asarray(x, np.float32).astype(ml_dtypes.bfloat16).astype(np.float64), axis, -1)
    blocks = v.reshape(v.shape[:-1] + (-1, 32))
    amax = np.abs(blocks).max(-1, keepdims=True)
    byte = np.maximum(np.where(amax > 0, np.frexp(amax)[1] - 1 + 127, 0) - down, 1)
    scale = np.exp2(byte - 127.0)
    codes = (blocks / scale).astype(np.float32).astype(dtype).astype(np.float64)
    return np.moveaxis((codes * scale).reshape(v.shape), -1, axis)


WIDE = False


def mx_kscale(k):
    if not WIDE:
        return np.ones(k)
    levels = np.array([10, -10, 5, -5, 0])
    a = np.random.permutation(np.resize(levels, k // 512 * 4)).reshape(k // 512, 4)
    idx = np.arange(k)
    return np.exp2(a[idx // 512, idx % 128 // 32])


BF16 = ml_dtypes.bfloat16


def bf(x):
    return np.asarray(x, np.float32).astype(BF16)


def f64(x):
    return np.asarray(x).astype(np.float64)


B, T, D, DEPTH, F = 4, 1024, 1024, 4, 32
L = 2 ** DEPTH
N = L - 1
LF = L * F


def sigmoid(v):
    return 1.0 / (1.0 + np.exp(-v))


def leaf_probs(c):
    probs = np.ones(c.shape[:-1] + (1,))
    for m in range(DEPTH):
        start = 2 ** m - 1
        cl = c[..., start:start + 2 ** m]
        probs = np.stack([probs * cl, probs * (1.0 - cl)], axis=-1)
        probs = probs.reshape(probs.shape[:-2] + (-1,))
    return probs


def setup_inputs():
    s = mx_kscale(D)
    t = mx_kscale(LF).reshape(L, F)
    return {"x": bf(np.random.standard_normal((B, T, D)) * s),
            "node_logits": bf(np.random.standard_normal((B, T, N)) * 1.5),
            "node_b": bf(np.random.standard_normal(N) * 0.5),
            "w1": bf(np.random.standard_normal((L, D, F)) / np.sqrt(D) / s[None, :, None] * t[:, None, :]),
            "b1": bf(np.random.standard_normal((L, F)) * 0.5 * t),
            "w2": bf(np.random.standard_normal((L, F, D)) * 2.0 / np.sqrt(F) / t[:, :, None])}


def reference(x, node_logits, node_b, w1, b1, w2):
    probs = leaf_probs(sigmoid(f64(node_logits) + f64(node_b)))
    w1f = f64(w1).transpose(1, 0, 2).reshape(D, LF)
    a = mxq(f64(x), 2, "e4m3") @ mxq(w1f, 0, "e4m3")
    h = np.maximum(a.reshape(B, T, L, F) + f64(b1), 0.0) * probs[..., None]
    return mxq(h.reshape(B, T, LF), 2, "e4m3") @ mxq(f64(w2).reshape(LF, D), 0, "e4m3")

@@ -1,0 +1,305 @@
+from contextlib import ExitStack
+
+import concourse.mybir as mybir
+from concourse.masks import make_identity
+
+F32 = mybir.dt.float32
+BF16 = mybir.dt.bfloat16
+U32 = mybir.dt.uint32
+U8 = mybir.dt.uint8
+FP8X4 = mybir.dt.float8_e4m3fn_x4
+ALU = mybir.AluOpType
+ACT = mybir.ActivationFunctionType
+
+P = 128
+PACK = 4
+TOKENS = 4096
+D = 1024
+DEPTH = 4
+LEAVES = 16
+NODES = 15
+HIDDEN = 32
+LF = LEAVES * HIDDEN
+PASSES = D // (P * PACK)
+BANK = 512
+ROUND = 512
+ROUNDS = TOKENS // ROUND
+TILES = ROUND // P
+REPEAT = P // LEAVES
+X_BUFS = 6
+STEPS = ROUNDS * PACK
+LAG = 6
+VECTOR_TILE = 1
+
+FLOPS = 2 * TOKENS * D * LF * 2
+
+
+def tile_fastfeedforwardnetwork_pa_t_kernel(tc, x, node_logits, node_b, w1, b1, w2, out):
+    nc = tc.nc
+    x_rounds = x.flatten_outer_dims().rearrange("(r p j) d -> r p (j d)", p=P, j=TILES)
+    out_rounds = out.flatten_outer_dims().rearrange("(r p j) e -> r p j e", p=P, j=TILES)
+
+    with ExitStack() as ctx:
+        keep = ctx.enter_context(tc.tile_pool(name="keep", bufs=1))
+        x_pool = ctx.enter_context(tc.tile_pool(name="x_pool", bufs=X_BUFS))
+        xg_pool = ctx.enter_context(tc.tile_pool(name="xg_pool", bufs=2))
+        xq_pool = ctx.enter_context(tc.tile_pool(name="xq_pool", bufs=3))
+        spread_pool = ctx.enter_context(tc.tile_pool(name="spread_pool", bufs=2))
+        h_pool = ctx.enter_context(tc.tile_pool(name="h_pool", bufs=2))
+        out_pool = ctx.enter_context(tc.tile_pool(name="out_pool", bufs=8))
+        xt_psum = ctx.enter_context(tc.psum_pool(name="xt_psum", bufs=3))
+        a_psum = ctx.enter_context(tc.psum_pool(name="a_psum", bufs=2))
+        o_psum = ctx.enter_context(tc.psum_pool(name="o_psum", bufs=3))
+        ctx.enter_context(tc.manual_schedule())
+
+        x_tiles = {}
+
+        def load_x(r):
+            x_raw = x_pool.tile([P, TILES, D], BF16)
+            nc.sync.dma_start(out=x_raw[:].rearrange("p j d -> p (j d)"), in_=x_rounds[r])
+            x_tiles[r] = x_raw
+
+        logits = keep.tile([P, ROUNDS, TILES * NODES], BF16)
+        nc.sync.dma_start(
+            out=logits[:],
+            in_=node_logits.flatten_outer_dims().rearrange("(r p j) n -> p r (j n)", p=P, j=TILES),
+        )
+        node_bias = keep.tile([P, NODES], BF16)
+        nc.sync.dma_start(out=node_bias[:], in_=node_b.partition_broadcast(P))
+        b1_bf = keep.tile([P, PACK], BF16)
+        nc.sync.dma_start(out=b1_bf[:], in_=b1.rearrange("l (f s) -> (l f) s", s=PACK))
+        load_x(0)
+        w1_raw = keep.tile([P, LEAVES, PASSES, PACK, HIDDEN // PACK, PACK], BF16)
+        half_leaves = LEAVES // 2
+        for l0 in range(0, LEAVES, half_leaves):
+            nc.sync.dma_start(
+                out=w1_raw[:, l0 : l0 + half_leaves].rearrange("p l g (u e) f s -> p (l g u) (e f s)", e=2),
+                in_=w1[l0 : l0 + half_leaves].rearrange("l (c p e) f -> p (l c) (e f)", p=P, e=2),
+            )
+        w2_raw = keep.tile([P, PACK, D], BF16)
+        nc.sync.dma_start(
+            out=w2_raw[:].rearrange("p s e -> p (s e)"),
+            in_=w2.rearrange("l (f s) e -> (l f) (s e)", s=PACK),
+        )
+        for r in range(1, X_BUFS):
+            load_x(r)
+
+        ident = keep.tile([P, P], F32)
+        make_identity(nc, ident[:])
+
+        toks = ROUNDS * TILES
+        gate_in = keep.tile([P, toks, NODES], F32)
+        nc.vector.tensor_tensor(
+            out=gate_in[:],
+            in0=logits[:].rearrange("p r (j n) -> p (r j) n", n=NODES),
+            in1=node_bias[:].unsqueeze(1).to_broadcast([P, toks, NODES]),
+            op=ALU.add,
+        )
+        gates = keep.tile([P, toks, NODES, 2], F32)
+        nc.scalar.activation(out=gates[:, :, :, 0], in_=gate_in[:], func=ACT.Sigmoid)
+        nc.scalar.activation(out=gates[:, :, :, 1], in_=gate_in[:], func=ACT.Sigmoid, scale=-1.0)
+        probs = gates[:, :, 0, :]
+        for level in range(1, DEPTH):
+            nodes = 2 ** level
+            first = nodes - 1
+            children = keep.tile([P, toks, nodes, 2], F32, name="children%d" % level)
+            nc.vector.tensor_tensor(
+                out=children[:],
+                in0=probs.unsqueeze(3).to_broadcast([P, toks, nodes, 2]),
+                in1=gates[:, :, first : first + nodes, :],
+                op=ALU.mult,
+            )
+            probs = children[:].rearrange("p i n s -> p i (n s)")
+
+        b1_col = keep.tile([P, PACK], F32)
+        nc.vector.tensor_copy(out=b1_col[:], in_=b1_bf[:])
+
+        xg_tiles = {}
+        xq_tiles = {}
+
+        def transpose_x(r):
+            x_words = x_tiles[r][:].bitcast(F32)
+            x_grouped = xg_pool.tile([P, PASSES, ROUND, PACK], BF16, align_bytes=64)
+            grouped_words = x_grouped[:].bitcast(F32)
+            for g in range(PASSES):
+                for half in range(2):
+                    xt = xt_psum.tile([P, 2, 2 * P], F32)
+                    for u in range(2):
+                        for jj in range(2):
+                            first_word = (2 * g + u) * P
+                            nc.tensor.transpose(
+                                xt[:, u, jj * P : (jj + 1) * P],
+                                x_words[:, 2 * half + jj, first_word : first_word + P],
+                                ident[:],
+                            )
+                    nc.scalar.copy(
+                        out=grouped_words[:, g, half * 2 * P : (half + 1) * 2 * P, :],
+                        in_=xt[:].rearrange("p u w -> p w u"),
+                    )
+            xg_tiles[r] = x_grouped
+            x_codes = xq_pool.tile([P, PASSES, ROUND], U32, align_bytes=64)
+            x_scales = xq_pool.tile([P, PASSES, ROUND], U8, align_bytes=64)
+            xq_tiles[r] = (x_codes, x_scales)
+
+        def quantise_x(r, g):
+            x_codes, x_scales = xq_tiles[r]
+            nc.vector.quantize_mx(
+                out=x_codes[:, g, :].bitcast(FP8X4),
+                scales=x_scales[:, g, :],
+                in_=xg_tiles[r][:, g].rearrange("p w t -> p (w t)"),
+            )
+
+        leaf_rows = keep.tile([P, ROUNDS, ROUND], F32)
+
+        def spread_probs(r):
+            spread = spread_pool.tile([P, TILES, LEAVES, REPEAT], F32)
+            nc.vector.tensor_copy(
+                out=spread[:],
+                in_=probs[:, r * TILES : (r + 1) * TILES, :].unsqueeze(3).to_broadcast([P, TILES, LEAVES, REPEAT]),
+            )
+            rows = o_psum.tile([P, BANK], F32, tag="o")
+            for j in range(TILES):
+                nc.tensor.transpose(
+                    rows[:, j * P : (j + 1) * P], spread[:, j].rearrange("p l c -> p (l c)"), ident[:]
+                )
+            nc.scalar.copy(out=leaf_rows[:, r, :], in_=rows[:])
+
+        w1_codes = keep.tile([P, PASSES, PACK, P], U32, align_bytes=64)
+        w1_scales = keep.tile([P, PASSES, PACK, P], U8, align_bytes=64)
+        w2_codes = keep.tile([P, D], U32, align_bytes=64)
+        w2_scales = keep.tile([P, D], U8, align_bytes=64)
+        w2_grouped = keep.tile([P, D, PACK], BF16, align_bytes=64)
+
+        def prepare_w1():
+            w1_grouped = keep.tile([P, PASSES, PACK, P, PACK], BF16, align_bytes=64)
+            for l0 in range(0, LEAVES, half_leaves):
+                for g in range(PASSES):
+                    for s in range(PACK):
+                        nc.vector.tensor_copy(
+                            out=w1_grouped[:, g, s, l0 * REPEAT : (l0 + half_leaves) * REPEAT, :].rearrange(
+                                "p (l f) t -> p l f t", l=half_leaves
+                            ),
+                            in_=w1_raw[:, l0 : l0 + half_leaves, g, :, :, s].rearrange("p l t f -> p l f t"),
+                        )
+            nc.vector.quantize_mx(
+                out=w1_codes[:].rearrange("p g s m -> p (g s m)").bitcast(FP8X4),
+                scales=w1_scales[:].rearrange("p g s m -> p (g s m)"),
+                in_=w1_grouped[:].rearrange("p g s m t -> p (g s m t)"),
+            )
+
+        def regroup_w2():
+            nc.vector.tensor_copy(
+                out=w2_grouped[:, 0:BANK, :], in_=w2_raw[:, :, 0:BANK].rearrange("p s e -> p e s")
+            )
+            nc.scalar.copy(out=w2_grouped[:, BANK:D, :], in_=w2_raw[:, :, BANK:D].rearrange("p s e -> p e s"))
+
+        def quantise_w2():
+            nc.vector.quantize_mx(
+                out=w2_codes[:].bitcast(FP8X4),
+                scales=w2_scales[:],
+                in_=w2_grouped[:].rearrange("p e s -> p (e s)"),
+            )
+
+        weighted_tiles = {}
+        h_grouped_tiles = {}
+        hq_tiles = {}
+
+        def hidden_sums(r, s):
+            if s == 0:
+                weighted = h_pool.tile([P, PACK, ROUND], F32)
+                weighted_tiles[r] = weighted
+            x_codes, x_scales = xq_tiles[r]
+            a = a_psum.tile([P, BANK], F32)
+            for g in range(PASSES):
+                nc.tensor.matmul_mx(
+                    out=a[:],
+                    lhsT=w1_codes[:, g, s, :].bitcast(FP8X4),
+                    lhsT_scale=w1_scales[:, g, s, :],
+                    rhs=x_codes[:, g, :].bitcast(FP8X4),
+                    rhs_scale=x_scales[:, g, :],
+                    start=(g == 0),
+                    stop=(g == PASSES - 1),
+                )
+            nc.vector.scalar_tensor_tensor(
+                out=weighted_tiles[r][:, s, :],
+                in0=a[:],
+                scalar=b1_col[:, s : s + 1],
+                in1=leaf_rows[:, r, :],
+                op0=ALU.add,
+                op1=ALU.mult,
+            )
+
+        def relu_hidden(r):
+            h_grouped = h_pool.tile([P, ROUND, PACK], BF16, align_bytes=64)
+            nc.vector.tensor_scalar(
+                out=h_grouped[:],
+                in0=weighted_tiles[r][:].rearrange("p s w -> p w s"),
+                scalar1=0.0,
+                scalar2=None,
+                op0=ALU.max,
+            )
+            h_grouped_tiles[r] = h_grouped
+
+        def quantise_hidden(r):
+            h_codes = h_pool.tile([P, ROUND], U32, align_bytes=64)
+            h_scales = h_pool.tile([P, ROUND], U8, align_bytes=64)
+            nc.vector.quantize_mx(
+                out=h_codes[:].bitcast(FP8X4),
+                scales=h_scales[:],
+                in_=h_grouped_tiles[r][:].rearrange("p w s -> p (w s)"),
+            )
+            hq_tiles[r] = (h_codes, h_scales)
+
+        def output_tile(r, j):
+            h_codes, h_scales = hq_tiles[r]
+            result = out_pool.tile([P, D], F32)
+            for half in range(D // BANK):
+                e0 = half * BANK
+                o = o_psum.tile([P, BANK], F32, tag="o")
+                nc.tensor.matmul_mx(
+                    out=o[:],
+                    lhsT=h_codes[:, j * P : (j + 1) * P].bitcast(FP8X4),
+                    lhsT_scale=h_scales[:, j * P : (j + 1) * P],
+                    rhs=w2_codes[:, e0 : e0 + BANK].bitcast(FP8X4),
+                    rhs_scale=w2_scales[:, e0 : e0 + BANK],
+                    start=True,
+                    stop=True,
+                )
+                if half == 1 and (j == VECTOR_TILE or r == ROUNDS - 1):
+                    nc.vector.tensor_copy(out=result[:, e0 : e0 + BANK], in_=o[:])
+                else:
+                    nc.scalar.copy(out=result[:, e0 : e0 + BANK], in_=o[:])
+            nc.sync.dma_start(out=out_rounds[r][:, j, :], in_=result[:])
+
+        transpose_x(0)
+        load_x(X_BUFS)
+        for r in range(ROUNDS):
+            spread_probs(r)
+        for g in range(PASSES):
+            quantise_x(0, g)
+        prepare_w1()
+        regroup_w2()
+        for s in range(PACK):
+            hidden_sums(0, s)
+        transpose_x(1)
+        load_x(X_BUFS + 1)
+        quantise_w2()
+        relu_hidden(0)
+        for g in range(PASSES):
+            quantise_x(1, g)
+        quantise_hidden(0)
+        transpose_x(2)
+        for step in range(PACK, STEPS + LAG):
+            r, s = divmod(step, PACK)
+            if r < ROUNDS:
+                hidden_sums(r, s)
+                if s < PASSES and r + 1 < ROUNDS:
+                    quantise_x(r + 1, s)
+            if step >= LAG:
+                done_round, j = divmod(step - LAG, TILES)
+                output_tile(done_round, j)
+            if r < ROUNDS and s == PACK - 1:
+                if r + 2 < ROUNDS:
+                    transpose_x(r + 2)
+                relu_hidden(r)
+                quantise_hidden(r)

@@ -29,6 +29,7 @@ REPEAT = P // LEAVES
 X_BUFS = 6
 STEPS = ROUNDS * PACK
 LAG = 6
+RUN = 4
 VECTOR_TILE = 1
 
 FLOPS = 2 * TOKENS * D * LF * 2
@@ -206,7 +207,7 @@ def tile_fastfeedforwardnetwork_pa_t_kernel(tc, x, node_logits, node_b, w1, b1, 
 
         def hidden_sums(r, s):
             if s == 0:
-                weighted = h_pool.tile([P, PACK, ROUND], F32)
+                weighted = h_pool.tile([P, PACK, ROUND], BF16)
                 weighted_tiles[r] = weighted
             x_codes, x_scales = xq_tiles[r]
             a = a_psum.tile([P, BANK], F32)
@@ -232,8 +233,8 @@ def tile_fastfeedforwardnetwork_pa_t_kernel(tc, x, node_logits, node_b, w1, b1, 
         def relu_hidden(r):
             h_grouped = h_pool.tile([P, ROUND, PACK], BF16, align_bytes=64)
             nc.vector.tensor_scalar(
-                out=h_grouped[:],
-                in0=weighted_tiles[r][:].rearrange("p s w -> p w s"),
+                out=h_grouped[:].rearrange("p (c i) s -> p c s i", i=RUN),
+                in0=weighted_tiles[r][:].rearrange("p s (c i) -> p c s i", i=RUN),
                 scalar1=0.0,
                 scalar2=None,
                 op0=ALU.max,

@@ -29,6 +29,10 @@ REPEAT = P // LEAVES
 X_BUFS = 6
 STEPS = ROUNDS * PACK
 LAG = 6
+AHEAD = 2
+X_PASSES = ROUNDS * PASSES
+W2_REGROUP_STEP = 1
+W2_QUANTISE_STEP = 3
 RUN = 4
 VECTOR_TILE = 1
 
@@ -48,9 +52,8 @@ def tile_fastfeedforwardnetwork_pa_t_kernel(tc, x, node_logits, node_b, w1, b1, 
         spread_pool = ctx.enter_context(tc.tile_pool(name="spread_pool", bufs=2))
         h_pool = ctx.enter_context(tc.tile_pool(name="h_pool", bufs=2))
         out_pool = ctx.enter_context(tc.tile_pool(name="out_pool", bufs=8))
-        xt_psum = ctx.enter_context(tc.psum_pool(name="xt_psum", bufs=3))
-        a_psum = ctx.enter_context(tc.psum_pool(name="a_psum", bufs=2))
-        o_psum = ctx.enter_context(tc.psum_pool(name="o_psum", bufs=3))
+        a_psum = ctx.enter_context(tc.psum_pool(name="a_psum", bufs=3))
+        turn_psum = ctx.enter_context(tc.psum_pool(name="turn_psum", bufs=5))
         ctx.enter_context(tc.manual_schedule())
 
         x_tiles = {}
@@ -77,12 +80,13 @@ def tile_fastfeedforwardnetwork_pa_t_kernel(tc, x, node_logits, node_b, w1, b1, 
                 out=w1_raw[:, l0 : l0 + half_leaves].rearrange("p l g (u e) f s -> p (l g u) (e f s)", e=2),
                 in_=w1[l0 : l0 + half_leaves].rearrange("l (c p e) f -> p (l c) (e f)", p=P, e=2),
             )
+        load_x(1)
         w2_raw = keep.tile([P, PACK, D], BF16)
         nc.sync.dma_start(
             out=w2_raw[:].rearrange("p s e -> p (s e)"),
             in_=w2.rearrange("l (f s) e -> (l f) (s e)", s=PACK),
         )
-        for r in range(1, X_BUFS):
+        for r in range(2, X_BUFS):
             load_x(r)
 
         ident = keep.tile([P, P], F32)
@@ -118,29 +122,29 @@ def tile_fastfeedforwardnetwork_pa_t_kernel(tc, x, node_logits, node_b, w1, b1, 
         xg_tiles = {}
         xq_tiles = {}
 
-        def transpose_x(r):
+        def transpose_x(r, g):
+            if g == 0:
+                x_grouped = xg_pool.tile([P, PASSES, ROUND, PACK], BF16, align_bytes=64)
+                x_codes = xq_pool.tile([P, PASSES, ROUND], U32, align_bytes=64)
+                x_scales = xq_pool.tile([P, PASSES, ROUND], U8, align_bytes=64)
+                xg_tiles[r] = x_grouped
+                xq_tiles[r] = (x_codes, x_scales)
             x_words = x_tiles[r][:].bitcast(F32)
-            x_grouped = xg_pool.tile([P, PASSES, ROUND, PACK], BF16, align_bytes=64)
-            grouped_words = x_grouped[:].bitcast(F32)
-            for g in range(PASSES):
-                for half in range(2):
-                    xt = xt_psum.tile([P, 2, 2 * P], F32)
-                    for u in range(2):
-                        for jj in range(2):
-                            first_word = (2 * g + u) * P
-                            nc.tensor.transpose(
-                                xt[:, u, jj * P : (jj + 1) * P],
-                                x_words[:, 2 * half + jj, first_word : first_word + P],
-                                ident[:],
-                            )
-                    nc.scalar.copy(
-                        out=grouped_words[:, g, half * 2 * P : (half + 1) * 2 * P, :],
-                        in_=xt[:].rearrange("p u w -> p w u"),
-                    )
-            xg_tiles[r] = x_grouped
-            x_codes = xq_pool.tile([P, PASSES, ROUND], U32, align_bytes=64)
-            x_scales = xq_pool.tile([P, PASSES, ROUND], U8, align_bytes=64)
-            xq_tiles[r] = (x_codes, x_scales)
+            grouped_words = xg_tiles[r][:].bitcast(F32)
+            for half in range(2):
+                xt = turn_psum.tile([P, 2, 2 * P], F32, tag="turn")
+                for u in range(2):
+                    for jj in range(2):
+                        first_word = (2 * g + u) * P
+                        nc.tensor.transpose(
+                            xt[:, u, jj * P : (jj + 1) * P],
+                            x_words[:, 2 * half + jj, first_word : first_word + P],
+                            ident[:],
+                        )
+                nc.scalar.copy(
+                    out=grouped_words[:, g, half * 2 * P : (half + 1) * 2 * P, :],
+                    in_=xt[:].rearrange("p u w -> p w u"),
+                )
 
         def quantise_x(r, g):
             x_codes, x_scales = xq_tiles[r]
@@ -158,7 +162,7 @@ def tile_fastfeedforwardnetwork_pa_t_kernel(tc, x, node_logits, node_b, w1, b1, 
                 out=spread[:],
                 in_=probs[:, r * TILES : (r + 1) * TILES, :].unsqueeze(3).to_broadcast([P, TILES, LEAVES, REPEAT]),
             )
-            rows = o_psum.tile([P, BANK], F32, tag="o")
+            rows = turn_psum.tile([P, BANK], F32, tag="turn")
             for j in range(TILES):
                 nc.tensor.transpose(
                     rows[:, j * P : (j + 1) * P], spread[:, j].rearrange("p l c -> p (l c)"), ident[:]
@@ -256,7 +260,7 @@ def tile_fastfeedforwardnetwork_pa_t_kernel(tc, x, node_logits, node_b, w1, b1, 
             result = out_pool.tile([P, D], F32)
             for half in range(D // BANK):
                 e0 = half * BANK
-                o = o_psum.tile([P, BANK], F32, tag="o")
+                o = turn_psum.tile([P, BANK], F32, tag="turn")
                 nc.tensor.matmul_mx(
                     out=o[:],
                     lhsT=h_codes[:, j * P : (j + 1) * P].bitcast(FP8X4),
@@ -272,35 +276,34 @@ def tile_fastfeedforwardnetwork_pa_t_kernel(tc, x, node_logits, node_b, w1, b1, 
                     nc.scalar.copy(out=result[:, e0 : e0 + BANK], in_=o[:])
             nc.sync.dma_start(out=out_rounds[r][:, j, :], in_=result[:])
 
-        transpose_x(0)
+        for g in range(PASSES):
+            transpose_x(0, g)
         load_x(X_BUFS)
         for r in range(ROUNDS):
             spread_probs(r)
         for g in range(PASSES):
             quantise_x(0, g)
         prepare_w1()
-        regroup_w2()
-        for s in range(PACK):
-            hidden_sums(0, s)
-        transpose_x(1)
+        for g in range(PASSES):
+            transpose_x(1, g)
         load_x(X_BUFS + 1)
-        quantise_w2()
-        relu_hidden(0)
         for g in range(PASSES):
             quantise_x(1, g)
-        quantise_hidden(0)
-        transpose_x(2)
-        for step in range(PACK, STEPS + LAG):
+        for step in range(STEPS + LAG):
             r, s = divmod(step, PACK)
-            if r < ROUNDS:
+            if step < STEPS:
                 hidden_sums(r, s)
-                if s < PASSES and r + 1 < ROUNDS:
-                    quantise_x(r + 1, s)
+            if step == W2_REGROUP_STEP:
+                regroup_w2()
+            if step == W2_QUANTISE_STEP:
+                quantise_w2()
+            x_pass = step // 2 + AHEAD * PASSES
+            if step % 2 == 0 and step > 0 and x_pass - 1 < X_PASSES:
+                quantise_x(*divmod(x_pass - 1, PASSES))
             if step >= LAG:
-                done_round, j = divmod(step - LAG, TILES)
-                output_tile(done_round, j)
-            if r < ROUNDS and s == PACK - 1:
-                if r + 2 < ROUNDS:
-                    transpose_x(r + 2)
+                output_tile(*divmod(step - LAG, TILES))
+            if step % 2 == 1 and x_pass < X_PASSES:
+                transpose_x(*divmod(x_pass, PASSES))
+            if step < STEPS and s == PACK - 1:
                 relu_hidden(r)
                 quantise_hidden(r)

@@ -34,7 +34,6 @@ X_PASSES = ROUNDS * PASSES
 W2_REGROUP_STEP = 1
 W2_QUANTISE_STEP = 3
 RUN = 4
-VECTOR_TILE = 1
 
 FLOPS = 2 * TOKENS * D * LF * 2
 
@@ -270,7 +269,7 @@ def tile_fastfeedforwardnetwork_pa_t_kernel(tc, x, node_logits, node_b, w1, b1, 
                     start=True,
                     stop=True,
                 )
-                if half == 1 and (j == VECTOR_TILE or r == ROUNDS - 1):
+                if half == 1 and (j % 2 == 1 or r == ROUNDS - 1):
                     nc.vector.tensor_copy(out=result[:, e0 : e0 + BANK], in_=o[:])
                 else:
                     nc.scalar.copy(out=result[:, e0 : e0 + BANK], in_=o[:])

@@ -34,6 +34,7 @@ X_PASSES = ROUNDS * PASSES
 W2_REGROUP_STEP = 1
 W2_QUANTISE_STEP = 3
 RUN = 4
+VECTOR_TILE = 3
 
 FLOPS = 2 * TOKENS * D * LF * 2
 
@@ -63,22 +64,23 @@ def tile_fastfeedforwardnetwork_pa_t_kernel(tc, x, node_logits, node_b, w1, b1, 
             x_tiles[r] = x_raw
 
         logits = keep.tile([P, ROUNDS, TILES * NODES], BF16)
-        nc.sync.dma_start(
+        nc.scalar.dma_start(
             out=logits[:],
             in_=node_logits.flatten_outer_dims().rearrange("(r p j) n -> p r (j n)", p=P, j=TILES),
         )
         node_bias = keep.tile([P, NODES], BF16)
-        nc.sync.dma_start(out=node_bias[:], in_=node_b.partition_broadcast(P))
+        nc.scalar.dma_start(out=node_bias[:], in_=node_b.partition_broadcast(P))
         b1_bf = keep.tile([P, PACK], BF16)
-        nc.sync.dma_start(out=b1_bf[:], in_=b1.rearrange("l (f s) -> (l f) s", s=PACK))
+        nc.scalar.dma_start(out=b1_bf[:], in_=b1.rearrange("l (f s) -> (l f) s", s=PACK))
         load_x(0)
         w1_raw = keep.tile([P, LEAVES, PASSES, PACK, HIDDEN // PACK, PACK], BF16)
-        half_leaves = LEAVES // 2
-        for l0 in range(0, LEAVES, half_leaves):
-            nc.sync.dma_start(
-                out=w1_raw[:, l0 : l0 + half_leaves].rearrange("p l g (u e) f s -> p (l g u) (e f s)", e=2),
-                in_=w1[l0 : l0 + half_leaves].rearrange("l (c p e) f -> p (l c) (e f)", p=P, e=2),
-            )
+        w1_chunks = w1.rearrange("l (c p e) f -> c p l (e f)", p=P, e=2)
+        for g in range(PASSES):
+            for u in range(2):
+                nc.sync.dma_start(
+                    out=w1_raw[:, :, g, 2 * u : 2 * u + 2, :, :].rearrange("p l t f s -> p l (t f s)"),
+                    in_=w1_chunks[2 * g + u],
+                )
         load_x(1)
         w2_raw = keep.tile([P, PACK, D], BF16)
         nc.sync.dma_start(
@@ -174,28 +176,29 @@ def tile_fastfeedforwardnetwork_pa_t_kernel(tc, x, node_logits, node_b, w1, b1, 
         w2_scales = keep.tile([P, D], U8, align_bytes=64)
         w2_grouped = keep.tile([P, D, PACK], BF16, align_bytes=64)
 
-        def prepare_w1():
-            w1_grouped = keep.tile([P, PASSES, PACK, P, PACK], BF16, align_bytes=64)
-            for l0 in range(0, LEAVES, half_leaves):
-                for g in range(PASSES):
-                    for s in range(PACK):
-                        nc.vector.tensor_copy(
-                            out=w1_grouped[:, g, s, l0 * REPEAT : (l0 + half_leaves) * REPEAT, :].rearrange(
-                                "p (l f) t -> p l f t", l=half_leaves
-                            ),
-                            in_=w1_raw[:, l0 : l0 + half_leaves, g, :, :, s].rearrange("p l t f -> p l f t"),
-                        )
+        w1_grouped = keep.tile([P, PASSES, PACK, P, PACK], BF16, align_bytes=64)
+
+        def prepare_w1(g):
+            for s in range(PACK):
+                nc.vector.tensor_copy(
+                    out=w1_grouped[:, g, s].rearrange("p (l f) t -> p l f t", l=LEAVES),
+                    in_=w1_raw[:, :, g, :, :, s].rearrange("p l t f -> p l f t"),
+                )
             nc.vector.quantize_mx(
-                out=w1_codes[:].rearrange("p g s m -> p (g s m)").bitcast(FP8X4),
-                scales=w1_scales[:].rearrange("p g s m -> p (g s m)"),
-                in_=w1_grouped[:].rearrange("p g s m t -> p (g s m t)"),
+                out=w1_codes[:, g].rearrange("p s m -> p (s m)").bitcast(FP8X4),
+                scales=w1_scales[:, g].rearrange("p s m -> p (s m)"),
+                in_=w1_grouped[:, g].rearrange("p s m t -> p (s m t)"),
             )
 
         def regroup_w2():
             nc.vector.tensor_copy(
-                out=w2_grouped[:, 0:BANK, :], in_=w2_raw[:, :, 0:BANK].rearrange("p s e -> p e s")
+                out=w2_grouped[:, 0:BANK, :].rearrange("p (c i) s -> p c s i", i=RUN),
+                in_=w2_raw[:, :, 0:BANK].rearrange("p s (c i) -> p c s i", i=RUN),
             )
-            nc.scalar.copy(out=w2_grouped[:, BANK:D, :], in_=w2_raw[:, :, BANK:D].rearrange("p s e -> p e s"))
+            nc.scalar.copy(
+                out=w2_grouped[:, BANK:D, :].rearrange("p (c i) s -> p c s i", i=RUN),
+                in_=w2_raw[:, :, BANK:D].rearrange("p s (c i) -> p c s i", i=RUN),
+            )
 
         def quantise_w2():
             nc.vector.quantize_mx(
@@ -269,7 +272,7 @@ def tile_fastfeedforwardnetwork_pa_t_kernel(tc, x, node_logits, node_b, w1, b1, 
                     start=True,
                     stop=True,
                 )
-                if half == 1 and (j % 2 == 1 or r == ROUNDS - 1):
+                if half == 1 and (j == VECTOR_TILE or r == ROUNDS - 1):
                     nc.vector.tensor_copy(out=result[:, e0 : e0 + BANK], in_=o[:])
                 else:
                     nc.scalar.copy(out=result[:, e0 : e0 + BANK], in_=o[:])
@@ -280,9 +283,10 @@ def tile_fastfeedforwardnetwork_pa_t_kernel(tc, x, node_logits, node_b, w1, b1, 
         load_x(X_BUFS)
         for r in range(ROUNDS):
             spread_probs(r)
+        prepare_w1(0)
         for g in range(PASSES):
             quantise_x(0, g)
-        prepare_w1()
+        prepare_w1(1)
         for g in range(PASSES):
             transpose_x(1, g)
         load_x(X_BUFS + 1)

from contextlib import ExitStack

import concourse.mybir as mybir
from concourse.masks import make_identity

F32 = mybir.dt.float32
BF16 = mybir.dt.bfloat16
U32 = mybir.dt.uint32
U8 = mybir.dt.uint8
FP8X4 = mybir.dt.float8_e4m3fn_x4
ALU = mybir.AluOpType
ACT = mybir.ActivationFunctionType

P = 128
PACK = 4
TOKENS = 4096
D = 1024
DEPTH = 4
LEAVES = 16
NODES = 15
HIDDEN = 32
LF = LEAVES * HIDDEN
PASSES = D // (P * PACK)
BANK = 512
ROUND = 512
ROUNDS = TOKENS // ROUND
TILES = ROUND // P
REPEAT = P // LEAVES
X_BUFS = 6
STEPS = ROUNDS * PACK
LAG = 6
AHEAD = 2
X_PASSES = ROUNDS * PASSES
W2_REGROUP_STEP = 1
W2_QUANTISE_STEP = 3
RUN = 4
VECTOR_TILE = 3

FLOPS = 2 * TOKENS * D * LF * 2


def tile_fastfeedforwardnetwork_pa_t_kernel(tc, x, node_logits, node_b, w1, b1, w2, out):
    nc = tc.nc
    x_rounds = x.flatten_outer_dims().rearrange("(r p j) d -> r p (j d)", p=P, j=TILES)
    out_rounds = out.flatten_outer_dims().rearrange("(r p j) e -> r p j e", p=P, j=TILES)

    with ExitStack() as ctx:
        keep = ctx.enter_context(tc.tile_pool(name="keep", bufs=1))
        x_pool = ctx.enter_context(tc.tile_pool(name="x_pool", bufs=X_BUFS))
        xg_pool = ctx.enter_context(tc.tile_pool(name="xg_pool", bufs=2))
        xq_pool = ctx.enter_context(tc.tile_pool(name="xq_pool", bufs=3))
        spread_pool = ctx.enter_context(tc.tile_pool(name="spread_pool", bufs=2))
        h_pool = ctx.enter_context(tc.tile_pool(name="h_pool", bufs=2))
        out_pool = ctx.enter_context(tc.tile_pool(name="out_pool", bufs=8))
        a_psum = ctx.enter_context(tc.psum_pool(name="a_psum", bufs=3))
        turn_psum = ctx.enter_context(tc.psum_pool(name="turn_psum", bufs=5))
        ctx.enter_context(tc.manual_schedule())

        x_tiles = {}

        def load_x(r):
            x_raw = x_pool.tile([P, TILES, D], BF16)
            nc.sync.dma_start(out=x_raw[:].rearrange("p j d -> p (j d)"), in_=x_rounds[r])
            x_tiles[r] = x_raw

        logits = keep.tile([P, ROUNDS, TILES * NODES], BF16)
        nc.scalar.dma_start(
            out=logits[:],
            in_=node_logits.flatten_outer_dims().rearrange("(r p j) n -> p r (j n)", p=P, j=TILES),
        )
        node_bias = keep.tile([P, NODES], BF16)
        nc.scalar.dma_start(out=node_bias[:], in_=node_b.partition_broadcast(P))
        b1_bf = keep.tile([P, PACK], BF16)
        nc.scalar.dma_start(out=b1_bf[:], in_=b1.rearrange("l (f s) -> (l f) s", s=PACK))
        load_x(0)
        w1_raw = keep.tile([P, LEAVES, PASSES, PACK, HIDDEN // PACK, PACK], BF16)
        w1_chunks = w1.rearrange("l (c p e) f -> c p l (e f)", p=P, e=2)
        for g in range(PASSES):
            for u in range(2):
                nc.sync.dma_start(
                    out=w1_raw[:, :, g, 2 * u : 2 * u + 2, :, :].rearrange("p l t f s -> p l (t f s)"),
                    in_=w1_chunks[2 * g + u],
                )
        load_x(1)
        w2_raw = keep.tile([P, PACK, D], BF16)
        nc.sync.dma_start(
            out=w2_raw[:].rearrange("p s e -> p (s e)"),
            in_=w2.rearrange("l (f s) e -> (l f) (s e)", s=PACK),
        )
        for r in range(2, X_BUFS):
            load_x(r)

        ident = keep.tile([P, P], F32)
        make_identity(nc, ident[:])

        toks = ROUNDS * TILES
        gate_in = keep.tile([P, toks, NODES], F32)
        nc.vector.tensor_tensor(
            out=gate_in[:],
            in0=logits[:].rearrange("p r (j n) -> p (r j) n", n=NODES),
            in1=node_bias[:].unsqueeze(1).to_broadcast([P, toks, NODES]),
            op=ALU.add,
        )
        gates = keep.tile([P, toks, NODES, 2], F32)
        nc.scalar.activation(out=gates[:, :, :, 0], in_=gate_in[:], func=ACT.Sigmoid)
        nc.scalar.activation(out=gates[:, :, :, 1], in_=gate_in[:], func=ACT.Sigmoid, scale=-1.0)
        probs = gates[:, :, 0, :]
        for level in range(1, DEPTH):
            nodes = 2 ** level
            first = nodes - 1
            children = keep.tile([P, toks, nodes, 2], F32, name="children%d" % level)
            nc.vector.tensor_tensor(
                out=children[:],
                in0=probs.unsqueeze(3).to_broadcast([P, toks, nodes, 2]),
                in1=gates[:, :, first : first + nodes, :],
                op=ALU.mult,
            )
            probs = children[:].rearrange("p i n s -> p i (n s)")

        b1_col = keep.tile([P, PACK], F32)
        nc.vector.tensor_copy(out=b1_col[:], in_=b1_bf[:])

        xg_tiles = {}
        xq_tiles = {}

        def transpose_x(r, g):
            if g == 0:
                x_grouped = xg_pool.tile([P, PASSES, ROUND, PACK], BF16, align_bytes=64)
                x_codes = xq_pool.tile([P, PASSES, ROUND], U32, align_bytes=64)
                x_scales = xq_pool.tile([P, PASSES, ROUND], U8, align_bytes=64)
                xg_tiles[r] = x_grouped
                xq_tiles[r] = (x_codes, x_scales)
            x_words = x_tiles[r][:].bitcast(F32)
            grouped_words = xg_tiles[r][:].bitcast(F32)
            for half in range(2):
                xt = turn_psum.tile([P, 2, 2 * P], F32, tag="turn")
                for u in range(2):
                    for jj in range(2):
                        first_word = (2 * g + u) * P
                        nc.tensor.transpose(
                            xt[:, u, jj * P : (jj + 1) * P],
                            x_words[:, 2 * half + jj, first_word : first_word + P],
                            ident[:],
                        )
                nc.scalar.copy(
                    out=grouped_words[:, g, half * 2 * P : (half + 1) * 2 * P, :],
                    in_=xt[:].rearrange("p u w -> p w u"),
                )

        def quantise_x(r, g):
            x_codes, x_scales = xq_tiles[r]
            nc.vector.quantize_mx(
                out=x_codes[:, g, :].bitcast(FP8X4),
                scales=x_scales[:, g, :],
                in_=xg_tiles[r][:, g].rearrange("p w t -> p (w t)"),
            )

        leaf_rows = keep.tile([P, ROUNDS, ROUND], F32)

        def spread_probs(r):
            spread = spread_pool.tile([P, TILES, LEAVES, REPEAT], F32)
            nc.vector.tensor_copy(
                out=spread[:],
                in_=probs[:, r * TILES : (r + 1) * TILES, :].unsqueeze(3).to_broadcast([P, TILES, LEAVES, REPEAT]),
            )
            rows = turn_psum.tile([P, BANK], F32, tag="turn")
            for j in range(TILES):
                nc.tensor.transpose(
                    rows[:, j * P : (j + 1) * P], spread[:, j].rearrange("p l c -> p (l c)"), ident[:]
                )
            nc.scalar.copy(out=leaf_rows[:, r, :], in_=rows[:])

        w1_codes = keep.tile([P, PASSES, PACK, P], U32, align_bytes=64)
        w1_scales = keep.tile([P, PASSES, PACK, P], U8, align_bytes=64)
        w2_codes = keep.tile([P, D], U32, align_bytes=64)
        w2_scales = keep.tile([P, D], U8, align_bytes=64)
        w2_grouped = keep.tile([P, D, PACK], BF16, align_bytes=64)

        w1_grouped = keep.tile([P, PASSES, PACK, P, PACK], BF16, align_bytes=64)

        def prepare_w1(g):
            for s in range(PACK):
                nc.vector.tensor_copy(
                    out=w1_grouped[:, g, s].rearrange("p (l f) t -> p l f t", l=LEAVES),
                    in_=w1_raw[:, :, g, :, :, s].rearrange("p l t f -> p l f t"),
                )
            nc.vector.quantize_mx(
                out=w1_codes[:, g].rearrange("p s m -> p (s m)").bitcast(FP8X4),
                scales=w1_scales[:, g].rearrange("p s m -> p (s m)"),
                in_=w1_grouped[:, g].rearrange("p s m t -> p (s m t)"),
            )

        def regroup_w2():
            nc.vector.tensor_copy(
                out=w2_grouped[:, 0:BANK, :].rearrange("p (c i) s -> p c s i", i=RUN),
                in_=w2_raw[:, :, 0:BANK].rearrange("p s (c i) -> p c s i", i=RUN),
            )
            nc.scalar.copy(
                out=w2_grouped[:, BANK:D, :].rearrange("p (c i) s -> p c s i", i=RUN),
                in_=w2_raw[:, :, BANK:D].rearrange("p s (c i) -> p c s i", i=RUN),
            )

        def quantise_w2():
            nc.vector.quantize_mx(
                out=w2_codes[:].bitcast(FP8X4),
                scales=w2_scales[:],
                in_=w2_grouped[:].rearrange("p e s -> p (e s)"),
            )

        weighted_tiles = {}
        h_grouped_tiles = {}
        hq_tiles = {}

        def hidden_sums(r, s):
            if s == 0:
                weighted = h_pool.tile([P, PACK, ROUND], BF16)
                weighted_tiles[r] = weighted
            x_codes, x_scales = xq_tiles[r]
            a = a_psum.tile([P, BANK], F32)
            for g in range(PASSES):
                nc.tensor.matmul_mx(
                    out=a[:],
                    lhsT=w1_codes[:, g, s, :].bitcast(FP8X4),
                    lhsT_scale=w1_scales[:, g, s, :],
                    rhs=x_codes[:, g, :].bitcast(FP8X4),
                    rhs_scale=x_scales[:, g, :],
                    start=(g == 0),
                    stop=(g == PASSES - 1),
                )
            nc.vector.scalar_tensor_tensor(
                out=weighted_tiles[r][:, s, :],
                in0=a[:],
                scalar=b1_col[:, s : s + 1],
                in1=leaf_rows[:, r, :],
                op0=ALU.add,
                op1=ALU.mult,
            )

        def relu_hidden(r):
            h_grouped = h_pool.tile([P, ROUND, PACK], BF16, align_bytes=64)
            nc.vector.tensor_scalar(
                out=h_grouped[:].rearrange("p (c i) s -> p c s i", i=RUN),
                in0=weighted_tiles[r][:].rearrange("p s (c i) -> p c s i", i=RUN),
                scalar1=0.0,
                scalar2=None,
                op0=ALU.max,
            )
            h_grouped_tiles[r] = h_grouped

        def quantise_hidden(r):
            h_codes = h_pool.tile([P, ROUND], U32, align_bytes=64)
            h_scales = h_pool.tile([P, ROUND], U8, align_bytes=64)
            nc.vector.quantize_mx(
                out=h_codes[:].bitcast(FP8X4),
                scales=h_scales[:],
                in_=h_grouped_tiles[r][:].rearrange("p w s -> p (w s)"),
            )
            hq_tiles[r] = (h_codes, h_scales)

        def output_tile(r, j):
            h_codes, h_scales = hq_tiles[r]
            result = out_pool.tile([P, D], F32)
            for half in range(D // BANK):
                e0 = half * BANK
                o = turn_psum.tile([P, BANK], F32, tag="turn")
                nc.tensor.matmul_mx(
                    out=o[:],
                    lhsT=h_codes[:, j * P : (j + 1) * P].bitcast(FP8X4),
                    lhsT_scale=h_scales[:, j * P : (j + 1) * P],
                    rhs=w2_codes[:, e0 : e0 + BANK].bitcast(FP8X4),
                    rhs_scale=w2_scales[:, e0 : e0 + BANK],
                    start=True,
                    stop=True,
                )
                if half == 1 and (j == VECTOR_TILE or r == ROUNDS - 1):
                    nc.vector.tensor_copy(out=result[:, e0 : e0 + BANK], in_=o[:])
                else:
                    nc.scalar.copy(out=result[:, e0 : e0 + BANK], in_=o[:])
            nc.sync.dma_start(out=out_rounds[r][:, j, :], in_=result[:])

        for g in range(PASSES):
            transpose_x(0, g)
        load_x(X_BUFS)
        for r in range(ROUNDS):
            spread_probs(r)
        prepare_w1(0)
        for g in range(PASSES):
            quantise_x(0, g)
        prepare_w1(1)
        for g in range(PASSES):
            transpose_x(1, g)
        load_x(X_BUFS + 1)
        for g in range(PASSES):
            quantise_x(1, g)
        for step in range(STEPS + LAG):
            r, s = divmod(step, PACK)
            if step < STEPS:
                hidden_sums(r, s)
            if step == W2_REGROUP_STEP:
                regroup_w2()
            if step == W2_QUANTISE_STEP:
                quantise_w2()
            x_pass = step // 2 + AHEAD * PASSES
            if step % 2 == 0 and step > 0 and x_pass - 1 < X_PASSES:
                quantise_x(*divmod(x_pass - 1, PASSES))
            if step >= LAG:
                output_tile(*divmod(step - LAG, TILES))
            if step % 2 == 1 and x_pass < X_PASSES:
                transpose_x(*divmod(x_pass, PASSES))
            if step < STEPS and s == PACK - 1:
                relu_hidden(r)
                quantise_hidden(r)
